import numpy as np
import ml_dtypes


def mxq(x, axis, fmt="e4m3"):
    dtype, down = {"e4m3": (ml_dtypes.float8_e4m3fn, 7), "e5m2": (ml_dtypes.float8_e5m2, 14)}[fmt]
    v = np.moveaxis(np.asarray(x, np.float32).astype(ml_dtypes.bfloat16).astype(np.float64), axis, -1)
    blocks = v.reshape(v.shape[:-1] + (-1, 32))
    amax = np.abs(blocks).max(-1, keepdims=True)
    byte = np.maximum(np.where(amax > 0, np.frexp(amax)[1] - 1 + 127, 0) - down, 1)
    scale = np.exp2(byte - 127.0)
    codes = (blocks / scale).astype(np.float32).astype(dtype).astype(np.float64)
    return np.moveaxis((codes * scale).reshape(v.shape), -1, axis)


WIDE = False


def mx_kscale(k):
    if not WIDE:
        return np.ones(k)
    levels = np.array([10, -10, 5, -5, 0])
    a = np.random.permutation(np.resize(levels, k // 512 * 4)).reshape(k // 512, 4)
    idx = np.arange(k)
    return np.exp2(a[idx // 512, idx % 128 // 32])


BF16 = ml_dtypes.bfloat16


def bf(x):
    return np.asarray(x, np.float32).astype(BF16)


def f64(x):
    return np.asarray(x).astype(np.float64)


B, H, S, D = 1, 4, 1024, 128
SIGMA_HS = np.array([5.0, 10.0, 20.0, 40.0])


def gaussian_prior(n_heads, len_q, len_k):
    i = np.arange(len_q)[:, None]
    j = np.arange(len_k)[None, :]
    diff2 = f64(j - i) ** 2
    sig2 = 2.0 * SIGMA_HS[:n_heads, None, None] ** 2
    gm = np.exp(-diff2[None, :, :] / sig2)
    return np.where((i >= j)[None, :, :], gm, 0.0)


def setup_inputs():
    s = mx_kscale(S)
    Q = np.random.standard_normal((B, H, S, D))
    K = np.random.standard_normal((B, H, S, D))
    V = np.random.standard_normal((B, H, S, D)) * 0.125 * np.sqrt(S)
    Q[..., 0] = np.log(2.0) * np.sqrt(D)
    K[..., 0] += np.log2(s)
    V = V / s[:, None] * np.mean(s)
    return {"Q": bf(Q), "K": bf(K), "V": bf(V),
            "attn_mask": np.random.random((B, H, S, S)) < 0.25}


def reference(Q, K, V, attn_mask):
    scores = f64(Q) @ f64(K).transpose(0, 1, 3, 2) / np.sqrt(D)
    scores = scores + gaussian_prior(H, S, S)[None]
    scores = np.where(np.asarray(attn_mask), -1e9, scores)
    e = np.exp(scores - scores.max(-1, keepdims=True))
    return (mxq(e, 3, "e4m3") @ mxq(f64(V), 2, "e4m3")) / e.sum(-1, keepdims=True)

@@ -1,0 +1,310 @@
+import math
+
+import concourse.mybir as mybir
+from concourse.masks import make_identity
+
+F32 = mybir.dt.float32
+BF16 = mybir.dt.bfloat16
+I32 = mybir.dt.int32
+U32 = mybir.dt.uint32
+U8 = mybir.dt.uint8
+FP8X4 = mybir.dt.float8_e4m3fn_x4
+ALU = mybir.AluOpType
+ACT = mybir.ActivationFunctionType
+
+P = 128
+H = 4
+S = 1024
+D = 128
+NB = S // P
+NBLK = H * NB
+SIGMA = (5.0, 10.0, 20.0, 40.0)
+FLOPS = 2 * 2 * H * S * S * D
+
+SCALE = 1.0 / math.sqrt(D)
+MASKED = -1.0e9 * math.sqrt(D)
+CUT = 30.0
+MASK_BUFS = 10
+GROUPS = (4, 4, 4, 4, 4, 4, 4, 2, 1, 1)
+
+
+def prior_deltas(h, pl):
+    keep = []
+    for delta in range(0, S, P):
+        low = delta - 254 - pl
+        if low <= 0 or low * low / (2.0 * SIGMA[h] ** 2) < CUT:
+            keep.append(delta)
+    return keep
+
+
+def tile_gpsdpattention_kernel(tc, Q, K, V, attn_mask, out):
+    nc = tc.nc
+
+    q_view = Q.rearrange("o h (p r) d -> p (o h) (r d)", p=P)
+    k_view = K.rearrange("o h (p r) d -> p (o h) (r d)", p=P)
+    v_view = V.rearrange("o h (g p r) d -> p (o h g) (r d)", p=P, r=4)
+    m_view = attn_mask.bitcast(I32).rearrange("o h (ib p) w -> p (o h ib) w", p=P)
+    o_view = out.rearrange("o h (ib p) d -> p (o h ib) d", p=P)
+
+    with tc.tile_pool(name="const", bufs=1) as const, tc.tile_pool(name="work", bufs=3) as work, tc.tile_pool(
+        name="masks", bufs=MASK_BUFS
+    ) as mask_pool, tc.psum_pool(name="ps_s", bufs=2) as ps_s, tc.psum_pool(name="ps_t", bufs=2) as ps_t, tc.psum_pool(
+        name="ps_o", bufs=2
+    ) as ps_o, tc.manual_schedule():
+        state = {}
+        k_raw = [const.tile([P, S], BF16, name="k_raw%d" % h) for h in range(H)]
+        q_raw = [const.tile([P, S], BF16, name="q_raw%d" % h) for h in range(H)]
+        v_raw = [const.tile([P, 2, 4 * D], BF16, name="v_raw%d" % h) for h in range(H)]
+
+        def load_mask(n):
+            mk = mask_pool.tile([P, 2 * S], I32, name="mk", tag="mk")
+            nc.sync.dma_start(out=mk[:], in_=m_view[:, n, :])
+            state[("mk", n)] = mk
+
+        def load_qk(h):
+            nc.sync.dma_start(out=k_raw[h][:], in_=k_view[:, h, :])
+            nc.sync.dma_start(out=q_raw[h][:], in_=q_view[:, h, :])
+            nc.sync.dma_start(out=v_raw[h][:], in_=v_view[:, 2 * h : 2 * h + 2, :])
+
+        nc.scalar.dma_start(out=k_raw[0][:], in_=k_view[:, 0, :])
+        nc.scalar.dma_start(out=q_raw[0][:], in_=q_view[:, 0, :])
+        load_mask(0)
+        nc.sync.dma_start(out=v_raw[0][:], in_=v_view[:, 0:2, :])
+        for n in range(1, 4):
+            load_mask(n)
+        load_qk(1)
+        for n in range(4, MASK_BUFS):
+            load_mask(n)
+
+        ident_b = const.tile([P, P], BF16, name="ident_b")
+        make_identity(nc, ident_b[:])
+        width = 644
+        dist = const.tile([P, width], F32, name="dist")
+        nc.gpsimd.iota(dist[:], pattern=[[1, width]], base=-1, channel_multiplier=-2, allow_small_or_imprecise_dtypes=True)
+        ident_f = const.tile([P, P], F32, name="ident_f")
+        make_identity(nc, ident_f[:])
+        dist_p = const.tile([P, width], F32, name="dist_p")
+        nc.vector.scalar_tensor_tensor(out=dist_p[:], in0=dist[:], scalar=-1.0e4, in1=dist[:], op0=ALU.mult, op1=ALU.max)
+        dist_2 = const.tile([P, width], F32, name="dist_2")
+        nc.scalar.activation(out=dist_2[:], in_=dist_p[:], func=ACT.Square)
+        prior = [const.tile([P, max(prior_deltas(h, 0)) + P + 1], F32, name="prior%d" % h) for h in range(H)]
+
+        def make_prior(h):
+            w_h = max(prior_deltas(h, 0)) + P + 1
+            nc.scalar.activation(out=prior[h][:], in_=dist_2[:, :w_h], func=ACT.Exp, scale=-1.0 / (2.0 * SIGMA[h] ** 2))
+            nc.gpsimd.tensor_scalar(
+                out=prior[h][:], in0=prior[h][:], scalar1=math.sqrt(D), scalar2=0.0, op0=ALU.mult, op1=ALU.add
+            )
+
+        neg_max = const.tile([P, NBLK], F32, name="neg_max")
+        row_sum = const.tile([P, NBLK], F32, name="row_sum")
+        row_inv = const.tile([P, NBLK], F32, name="row_inv")
+        junk = const.tile([P, S], F32, name="junk")
+
+        v_grp = [const.tile([P, 2, D, 4], BF16, name="v_grp%d" % h, align_bytes=64) for h in range(H)]
+        v_code = [const.tile([P, 2 * D], U32, name="v_code%d" % h, align_bytes=64) for h in range(H)]
+        v_scale = [const.tile([P, 2 * D], U8, name="v_scale%d" % h, align_bytes=64) for h in range(H)]
+
+        def regroup_v(h):
+            for g in range(2):
+                nc.gpsimd.tensor_scalar(
+                    out=v_grp[h][:, g, :, :].rearrange("p d (u e) -> p d u e", u=2),
+                    in0=v_raw[h][:, g, :].rearrange("p (e u d) -> p d u e", e=2, u=2),
+                    scalar1=1.0,
+                    scalar2=0.0,
+                    op0=ALU.mult,
+                    op1=ALU.add,
+                )
+
+        def quantise_v(h):
+            nc.vector.quantize_mx(
+                out=v_code[h][:].bitcast(FP8X4),
+                scales=v_scale[h][:],
+                in_=v_grp[h][:].rearrange("p g d t -> p (g d t)"),
+            )
+
+        q_t = [const.tile([P, S], BF16, name="q_t%d" % h) for h in range(H)]
+        k_t = [const.tile([P, S], BF16, name="k_t%d" % h) for h in range(H)]
+
+        def prep_qk(h):
+            pk = ps_t.tile([P, S], BF16, name="pk", tag="t")
+            for r in range(8):
+                nc.tensor.transpose(pk[:, r * P : (r + 1) * P], k_raw[h][:, r * D : (r + 1) * D], ident_b[:])
+            nc.vector.tensor_copy(
+                out=k_t[h][:].rearrange("d (pl p r2) -> d pl p r2", pl=2, r2=4),
+                in_=pk[:].rearrange("d (r2 pl p) -> d pl p r2", r2=4, pl=2),
+            )
+            pq = ps_t.tile([P, S], BF16, name="pq", tag="t")
+            for r in range(8):
+                nc.tensor.transpose(pq[:, r * P : (r + 1) * P], q_raw[h][:, r * D : (r + 1) * D], ident_b[:])
+            nc.scalar.copy(
+                out=q_t[h][:].rearrange("d (p r) -> d p r", r=8),
+                in_=pq[:].rearrange("d (r p) -> d p r", r=8),
+            )
+
+        def scores(n):
+            h, ib = divmod(n, NB)
+            banks = []
+            for pl in range(2):
+                ps = ps_s.tile([P, 512], F32, name="ps%d" % pl, tag="s%d" % pl)
+                adds = [b for b in range(4) if (P * ib - 2 * P * b) in prior_deltas(h, pl)]
+                nc.tensor.matmul(
+                    ps[:],
+                    lhsT=q_t[h][:, ib * P : (ib + 1) * P],
+                    rhs=k_t[h][:, pl * 512 : (pl + 1) * 512],
+                    start=True,
+                    stop=False,
+                )
+                for b in adds:
+                    x0 = P * ib - 2 * P * b - pl + 1
+                    nc.tensor.matmul(
+                        ps[:, b * P : (b + 1) * P],
+                        lhsT=prior[h][:, x0 : x0 + P],
+                        rhs=ident_f[:],
+                        is_transpose=True,
+                        start=False,
+                        stop=(b == adds[-1]),
+                    )
+                banks.append(ps)
+            state[("ps", n)] = banks
+
+        def masked(n):
+            st = work.tile([P, S], F32, name="st", tag="st")
+            low_words = state[("mk", n)][:].rearrange("p (c f) -> p c f", f=4)
+            for pl in range(2):
+                nc.vector.scalar_tensor_tensor(
+                    out=st[:, pl * 512 : (pl + 1) * 512],
+                    in0=low_words[:, :, 2 * pl],
+                    scalar=MASKED,
+                    in1=state[("ps", n)][pl][:],
+                    op0=ALU.mult,
+                    op1=ALU.add,
+                )
+            state[("st", n)] = st
+
+        def row_max(n):
+            nc.vector.tensor_scalar(
+                out=junk[:],
+                in0=state[("st", n)][:],
+                scalar1=-SCALE,
+                scalar2=None,
+                op0=ALU.mult,
+                op1=ALU.min,
+                accum_out=neg_max[:, n : n + 1],
+            )
+
+        def exps(n):
+            et = work.tile([P, S], BF16, name="et", tag="et")
+            nc.scalar.activation(
+                out=et[:],
+                in_=state[("st", n)][:],
+                func=ACT.Exp,
+                bias=neg_max[:, n : n + 1],
+                scale=SCALE,
+                accum_out=row_sum[:, n : n + 1],
+            )
+            state[("et", n)] = et
+
+        def flip(n):
+            pt = ps_t.tile([P, 4, P], F32, name="pt", tag="t")
+            words = state[("et", n)][:].bitcast(F32)
+            for beta in range(4):
+                nc.tensor.transpose(pt[:, beta, :], words[:, beta * P : (beta + 1) * P], ident_f[:])
+            state[("pt", n)] = pt
+
+        def regroup(n):
+            gt = work.tile([P, 2, P, 2], F32, name="gt", tag="gt", bufs=4, align_bytes=64)
+            nc.scalar.copy(out=gt[:], in_=state[("pt", n)][:].rearrange("p (u g) i -> p g i u", u=2))
+            state[("gt", n)] = gt
+
+        def quant(n):
+            cd = work.tile([P, 2 * P], U32, name="cd", tag="cd", align_bytes=64)
+            sc = work.tile([P, 2 * P], U8, name="sc", tag="sc", align_bytes=64)
+            nc.vector.quantize_mx(
+                out=cd[:].bitcast(FP8X4),
+                scales=sc[:],
+                in_=state[("gt", n)][:].rearrange("p g i u -> p (g i u)").bitcast(BF16),
+            )
+            state[("cd", n)] = (cd, sc)
+
+        group_of = {}
+        first = 0
+        for gi, size in enumerate(GROUPS):
+            for k in range(size):
+                group_of[first + k] = (gi, first, size, k)
+            first += size
+        finished = []
+
+        def weighted(n):
+            h = n // NB
+            gi, n0, size, k = group_of[n]
+            if k == 0:
+                state["po"] = ps_o.tile([P, 4, D], F32, name="po", tag="o")
+            po = state["po"]
+            cd, sc = state[("cd", n)]
+            for g in range(2):
+                nc.tensor.matmul_mx(
+                    out=po[:, k, :],
+                    lhsT=cd[:, g * P : (g + 1) * P].bitcast(FP8X4),
+                    lhsT_scale=sc[:, g * P : (g + 1) * P],
+                    rhs=v_code[h][:, g * D : (g + 1) * D].bitcast(FP8X4),
+                    rhs_scale=v_scale[h][:, g * D : (g + 1) * D],
+                    start=(g == 0),
+                    stop=(g == 1),
+                )
+
+        def finish(n):
+            gi, n0, size, k = group_of[n]
+            if k != size - 1:
+                return
+            po = state["po"]
+            nc.vector.reciprocal(out=row_inv[:, n0 : n0 + size], in_=row_sum[:, n0 : n0 + size])
+            ot = const.tile([P, size, D], F32, name="ot%d" % gi)
+            for j in range(size):
+                nc.scalar.activation(
+                    out=ot[:, j, :], in_=po[:, j, :], func=ACT.Copy, scale=row_inv[:, n0 + j : n0 + j + 1]
+                )
+            finished.append((n0, size, ot))
+
+        make_prior(0)
+        prep_qk(0)
+        regroup_v(0)
+        scores(0)
+        stored = 0
+        for t in range(NBLK + 3):
+            if t + 1 < NBLK:
+                scores(t + 1)
+            if t < NBLK:
+                masked(t)
+                nxt = t + MASK_BUFS
+                if nxt < NBLK:
+                    if nxt % NB == NB - 4 and nxt // NB + 1 < H:
+                        load_qk(nxt // NB + 1)
+                    load_mask(nxt)
+            if 0 <= t - 1 < NBLK:
+                flip(t - 1)
+            if 0 <= t - 3:
+                quant(t - 3)
+                weighted(t - 3)
+            if t < NBLK:
+                row_max(t)
+                exps(t)
+            if 0 <= t - 1 < NBLK:
+                regroup(t - 1)
+            if 0 <= t - 3:
+                finish(t - 3)
+            if t == 0:
+                quantise_v(0)
+            if t + 1 < H:
+                make_prior(t + 1)
+            h_next = (t + 5) // NB
+            if 0 < h_next < H:
+                if (t + 5) % NB == 0:
+                    regroup_v(h_next)
+                if (t + 5) % NB == 2:
+                    quantise_v(h_next)
+                    prep_qk(h_next)
+            if t + MASK_BUFS >= NBLK - 1:
+                for n0, size, ot in finished[stored:]:
+                    nc.sync.dma_start(out=o_view[:, n0 : n0 + size, :], in_=ot[:])
+                stored = len(finished)

@@ -28,10 +28,10 @@ MASK_BUFS = 10
 GROUPS = (4, 4, 4, 4, 4, 4, 4, 2, 1, 1)
 
 
-def prior_deltas(h, pl):
+def prior_deltas(h):
     keep = []
     for delta in range(0, S, P):
-        low = delta - 254 - pl
+        low = delta - (P - 1)
         if low <= 0 or low * low / (2.0 * SIGMA[h] ** 2) < CUT:
             keep.append(delta)
     return keep
@@ -42,7 +42,7 @@ def tile_gpsdpattention_kernel(tc, Q, K, V, attn_mask, out):
 
     q_view = Q.rearrange("o h (p r) d -> p (o h) (r d)", p=P)
     k_view = K.rearrange("o h (p r) d -> p (o h) (r d)", p=P)
-    v_view = V.rearrange("o h (g p r) d -> p (o h g) (r d)", p=P, r=4)
+    v_view = V.rearrange("o h (a p e) d -> p (o h a) (e d)", p=P, e=2)
     m_view = attn_mask.bitcast(I32).rearrange("o h (ib p) w -> p (o h ib) w", p=P)
     o_view = out.rearrange("o h (ib p) d -> p (o h ib) d", p=P)
 
@@ -54,7 +54,7 @@ def tile_gpsdpattention_kernel(tc, Q, K, V, attn_mask, out):
         state = {}
         k_raw = [const.tile([P, S], BF16, name="k_raw%d" % h) for h in range(H)]
         q_raw = [const.tile([P, S], BF16, name="q_raw%d" % h) for h in range(H)]
-        v_raw = [const.tile([P, 2, 4 * D], BF16, name="v_raw%d" % h) for h in range(H)]
+        v_raw = [const.tile([P, 4, 2 * D], BF16, name="v_raw%d" % h) for h in range(H)]
 
         def load_mask(n):
             mk = mask_pool.tile([P, 2 * S], I32, name="mk", tag="mk")
@@ -64,12 +64,12 @@ def tile_gpsdpattention_kernel(tc, Q, K, V, attn_mask, out):
         def load_qk(h):
             nc.sync.dma_start(out=k_raw[h][:], in_=k_view[:, h, :])
             nc.sync.dma_start(out=q_raw[h][:], in_=q_view[:, h, :])
-            nc.sync.dma_start(out=v_raw[h][:], in_=v_view[:, 2 * h : 2 * h + 2, :])
+            nc.sync.dma_start(out=v_raw[h][:], in_=v_view[:, 4 * h : 4 * h + 4, :])
 
         nc.scalar.dma_start(out=k_raw[0][:], in_=k_view[:, 0, :])
         nc.scalar.dma_start(out=q_raw[0][:], in_=q_view[:, 0, :])
         load_mask(0)
-        nc.sync.dma_start(out=v_raw[0][:], in_=v_view[:, 0:2, :])
+        nc.sync.dma_start(out=v_raw[0][:], in_=v_view[:, 0:4, :])
         for n in range(1, 4):
             load_mask(n)
         load_qk(1)
@@ -78,19 +78,19 @@ def tile_gpsdpattention_kernel(tc, Q, K, V, attn_mask, out):
 
         ident_b = const.tile([P, P], BF16, name="ident_b")
         make_identity(nc, ident_b[:])
-        width = 644
+        width = max(prior_deltas(H - 1)) + P
         dist = const.tile([P, width], F32, name="dist")
-        nc.gpsimd.iota(dist[:], pattern=[[1, width]], base=-1, channel_multiplier=-2, allow_small_or_imprecise_dtypes=True)
+        nc.gpsimd.iota(dist[:], pattern=[[1, width]], base=0, channel_multiplier=-1, allow_small_or_imprecise_dtypes=True)
         ident_f = const.tile([P, P], F32, name="ident_f")
         make_identity(nc, ident_f[:])
         dist_p = const.tile([P, width], F32, name="dist_p")
         nc.vector.scalar_tensor_tensor(out=dist_p[:], in0=dist[:], scalar=-1.0e4, in1=dist[:], op0=ALU.mult, op1=ALU.max)
         dist_2 = const.tile([P, width], F32, name="dist_2")
         nc.scalar.activation(out=dist_2[:], in_=dist_p[:], func=ACT.Square)
-        prior = [const.tile([P, max(prior_deltas(h, 0)) + P + 1], F32, name="prior%d" % h) for h in range(H)]
+        prior = [const.tile([P, max(prior_deltas(h)) + P], F32, name="prior%d" % h) for h in range(H)]
 
         def make_prior(h):
-            w_h = max(prior_deltas(h, 0)) + P + 1
+            w_h = max(prior_deltas(h)) + P
             nc.scalar.activation(out=prior[h][:], in_=dist_2[:, :w_h], func=ACT.Exp, scale=-1.0 / (2.0 * SIGMA[h] ** 2))
             nc.gpsimd.tensor_scalar(
                 out=prior[h][:], in0=prior[h][:], scalar1=math.sqrt(D), scalar2=0.0, op0=ALU.mult, op1=ALU.add
@@ -109,7 +109,7 @@ def tile_gpsdpattention_kernel(tc, Q, K, V, attn_mask, out):
             for g in range(2):
                 nc.gpsimd.tensor_scalar(
                     out=v_grp[h][:, g, :, :].rearrange("p d (u e) -> p d u e", u=2),
-                    in0=v_raw[h][:, g, :].rearrange("p (e u d) -> p d u e", e=2, u=2),
+                    in0=v_raw[h][:, 2 * g : 2 * g + 2, :].rearrange("p u (e d) -> p d u e", e=2),
                     scalar1=1.0,
                     scalar2=0.0,
                     op0=ALU.mult,
@@ -130,9 +130,9 @@ def tile_gpsdpattention_kernel(tc, Q, K, V, attn_mask, out):
             pk = ps_t.tile([P, S], BF16, name="pk", tag="t")
             for r in range(8):
                 nc.tensor.transpose(pk[:, r * P : (r + 1) * P], k_raw[h][:, r * D : (r + 1) * D], ident_b[:])
-            nc.vector.tensor_copy(
-                out=k_t[h][:].rearrange("d (pl p r2) -> d pl p r2", pl=2, r2=4),
-                in_=pk[:].rearrange("d (r2 pl p) -> d pl p r2", r2=4, pl=2),
+            nc.scalar.copy(
+                out=k_t[h][:].rearrange("d (p r) -> d p r", r=8),
+                in_=pk[:].rearrange("d (r p) -> d p r", r=8),
             )
             pq = ps_t.tile([P, S], BF16, name="pq", tag="t")
             for r in range(8):
@@ -147,16 +147,16 @@ def tile_gpsdpattention_kernel(tc, Q, K, V, attn_mask, out):
             banks = []
             for pl in range(2):
                 ps = ps_s.tile([P, 512], F32, name="ps%d" % pl, tag="s%d" % pl)
-                adds = [b for b in range(4) if (P * ib - 2 * P * b) in prior_deltas(h, pl)]
+                adds = [b for b in range(4) if P * (ib - 4 * pl - b) in prior_deltas(h)]
                 nc.tensor.matmul(
                     ps[:],
                     lhsT=q_t[h][:, ib * P : (ib + 1) * P],
                     rhs=k_t[h][:, pl * 512 : (pl + 1) * 512],
                     start=True,
-                    stop=False,
+                    stop=(len(adds) == 0),
                 )
                 for b in adds:
-                    x0 = P * ib - 2 * P * b - pl + 1
+                    x0 = P * (ib - 4 * pl - b)
                     nc.tensor.matmul(
                         ps[:, b * P : (b + 1) * P],
                         lhsT=prior[h][:, x0 : x0 + P],
@@ -170,11 +170,11 @@ def tile_gpsdpattention_kernel(tc, Q, K, V, attn_mask, out):
 
         def masked(n):
             st = work.tile([P, S], F32, name="st", tag="st")
-            low_words = state[("mk", n)][:].rearrange("p (c f) -> p c f", f=4)
+            low_words = state[("mk", n)][:].rearrange("p (c f) -> p c f", f=2)
             for pl in range(2):
                 nc.vector.scalar_tensor_tensor(
                     out=st[:, pl * 512 : (pl + 1) * 512],
-                    in0=low_words[:, :, 2 * pl],
+                    in0=low_words[:, pl * 512 : (pl + 1) * 512, 0],
                     scalar=MASKED,
                     in1=state[("ps", n)][pl][:],
                     op0=ALU.mult,
@@ -214,7 +214,7 @@ def tile_gpsdpattention_kernel(tc, Q, K, V, attn_mask, out):
 
         def regroup(n):
             gt = work.tile([P, 2, P, 2], F32, name="gt", tag="gt", bufs=4, align_bytes=64)
-            nc.scalar.copy(out=gt[:], in_=state[("pt", n)][:].rearrange("p (u g) i -> p g i u", u=2))
+            nc.scalar.copy(out=gt[:], in_=state[("pt", n)][:].rearrange("p (g u) i -> p g i u", u=2))
             state[("gt", n)] = gt
 
         def quant(n):

@@ -40,8 +40,8 @@ def prior_deltas(h):
 def tile_gpsdpattention_kernel(tc, Q, K, V, attn_mask, out):
     nc = tc.nc
 
-    q_view = Q.rearrange("o h (p r) d -> p (o h) (r d)", p=P)
-    k_view = K.rearrange("o h (p r) d -> p (o h) (r d)", p=P)
+    q_view = Q.rearrange("o h (b p) d -> p (o h b) d", p=P)
+    k_view = K.rearrange("o h (b p) d -> p (o h b) d", p=P)
     v_view = V.rearrange("o h (a p e) d -> p (o h a) (e d)", p=P, e=2)
     m_view = attn_mask.bitcast(I32).rearrange("o h (ib p) w -> p (o h ib) w", p=P)
     o_view = out.rearrange("o h (ib p) d -> p (o h ib) d", p=P)
@@ -52,8 +52,8 @@ def tile_gpsdpattention_kernel(tc, Q, K, V, attn_mask, out):
         name="ps_o", bufs=2
     ) as ps_o, tc.manual_schedule():
         state = {}
-        k_raw = [const.tile([P, S], BF16, name="k_raw%d" % h) for h in range(H)]
-        q_raw = [const.tile([P, S], BF16, name="q_raw%d" % h) for h in range(H)]
+        k_raw = [const.tile([P, NB, D], BF16, name="k_raw%d" % h) for h in range(H)]
+        q_raw = [const.tile([P, NB, D], BF16, name="q_raw%d" % h) for h in range(H)]
         v_raw = [const.tile([P, 4, 2 * D], BF16, name="v_raw%d" % h) for h in range(H)]
 
         def load_mask(n):
@@ -62,18 +62,18 @@ def tile_gpsdpattention_kernel(tc, Q, K, V, attn_mask, out):
             state[("mk", n)] = mk
 
         def load_qk(h):
-            nc.sync.dma_start(out=k_raw[h][:], in_=k_view[:, h, :])
-            nc.sync.dma_start(out=q_raw[h][:], in_=q_view[:, h, :])
+            nc.sync.dma_start(out=k_raw[h][:], in_=k_view[:, NB * h : NB * (h + 1), :])
+            nc.sync.dma_start(out=q_raw[h][:], in_=q_view[:, NB * h : NB * (h + 1), :])
             nc.sync.dma_start(out=v_raw[h][:], in_=v_view[:, 4 * h : 4 * h + 4, :])
 
-        nc.scalar.dma_start(out=k_raw[0][:], in_=k_view[:, 0, :])
-        nc.scalar.dma_start(out=q_raw[0][:], in_=q_view[:, 0, :])
+        nc.sync.dma_start(out=k_raw[0][:], in_=k_view[:, 0:NB, :])
+        nc.scalar.dma_start(out=q_raw[0][:], in_=q_view[:, 0:NB, :])
         load_mask(0)
         nc.sync.dma_start(out=v_raw[0][:], in_=v_view[:, 0:4, :])
-        for n in range(1, 4):
+        for n in range(1, 3):
             load_mask(n)
         load_qk(1)
-        for n in range(4, MASK_BUFS):
+        for n in range(3, MASK_BUFS):
             load_mask(n)
 
         ident_b = const.tile([P, P], BF16, name="ident_b")
@@ -92,9 +92,14 @@ def tile_gpsdpattention_kernel(tc, Q, K, V, attn_mask, out):
         def make_prior(h):
             w_h = max(prior_deltas(h)) + P
             nc.scalar.activation(out=prior[h][:], in_=dist_2[:, :w_h], func=ACT.Exp, scale=-1.0 / (2.0 * SIGMA[h] ** 2))
-            nc.gpsimd.tensor_scalar(
-                out=prior[h][:], in0=prior[h][:], scalar1=math.sqrt(D), scalar2=0.0, op0=ALU.mult, op1=ALU.add
-            )
+            if h == 0:
+                nc.vector.tensor_scalar(
+                    out=prior[h][:], in0=prior[h][:], scalar1=math.sqrt(D), scalar2=None, op0=ALU.mult
+                )
+            else:
+                nc.gpsimd.tensor_scalar(
+                    out=prior[h][:], in0=prior[h][:], scalar1=math.sqrt(D), scalar2=0.0, op0=ALU.mult, op1=ALU.add
+                )
 
         neg_max = const.tile([P, NBLK], F32, name="neg_max")
         row_sum = const.tile([P, NBLK], F32, name="row_sum")
@@ -126,21 +131,14 @@ def tile_gpsdpattention_kernel(tc, Q, K, V, attn_mask, out):
         q_t = [const.tile([P, S], BF16, name="q_t%d" % h) for h in range(H)]
         k_t = [const.tile([P, S], BF16, name="k_t%d" % h) for h in range(H)]
 
-        def prep_qk(h):
-            pk = ps_t.tile([P, S], BF16, name="pk", tag="t")
-            for r in range(8):
-                nc.tensor.transpose(pk[:, r * P : (r + 1) * P], k_raw[h][:, r * D : (r + 1) * D], ident_b[:])
-            nc.scalar.copy(
-                out=k_t[h][:].rearrange("d (p r) -> d p r", r=8),
-                in_=pk[:].rearrange("d (r p) -> d p r", r=8),
-            )
-            pq = ps_t.tile([P, S], BF16, name="pq", tag="t")
-            for r in range(8):
-                nc.tensor.transpose(pq[:, r * P : (r + 1) * P], q_raw[h][:, r * D : (r + 1) * D], ident_b[:])
-            nc.scalar.copy(
-                out=q_t[h][:].rearrange("d (p r) -> d p r", r=8),
-                in_=pq[:].rearrange("d (r p) -> d p r", r=8),
-            )
+        def flip_in(raw, dst, half, on_vector):
+            pin = ps_t.tile([P, 512], BF16, name="pin", tag="t")
+            for b in range(4):
+                nc.tensor.transpose(pin[:, b * P : (b + 1) * P], raw[:, 4 * half + b, :], ident_b[:])
+            if on_vector:
+                nc.vector.tensor_copy(out=dst[:, 512 * half : 512 * (half + 1)], in_=pin[:])
+            else:
+                nc.scalar.copy(out=dst[:, 512 * half : 512 * (half + 1)], in_=pin[:])
 
         def scores(n):
             h, ib = divmod(n, NB)
@@ -267,9 +265,12 @@ def tile_gpsdpattention_kernel(tc, Q, K, V, attn_mask, out):
             finished.append((n0, size, ot))
 
         make_prior(0)
-        prep_qk(0)
+        flip_in(k_raw[0], k_t[0], 0, True)
+        flip_in(q_raw[0], q_t[0], 0, False)
+        flip_in(k_raw[0], k_t[0], 1, True)
         regroup_v(0)
         scores(0)
+        flip_in(q_raw[0], q_t[0], 1, False)
         stored = 0
         for t in range(NBLK + 3):
             if t + 1 < NBLK:
@@ -303,7 +304,12 @@ def tile_gpsdpattention_kernel(tc, Q, K, V, attn_mask, out):
                     regroup_v(h_next)
                 if (t + 5) % NB == 2:
                     quantise_v(h_next)
-                    prep_qk(h_next)
+            h_flip, piece = divmod(t + 5, NB)
+            if 0 < h_flip < H and piece < 4:
+                if piece % 2 == 0:
+                    flip_in(k_raw[h_flip], k_t[h_flip], piece // 2, False)
+                else:
+                    flip_in(q_raw[h_flip], q_t[h_flip], piece // 2, False)
             if t + MASK_BUFS >= NBLK - 1:
                 for n0, size, ot in finished[stored:]:
                     nc.sync.dma_start(out=o_view[:, n0 : n0 + size, :], in_=ot[:])

@@ -107,8 +107,10 @@ def tile_gpsdpattention_kernel(tc, Q, K, V, attn_mask, out):
         junk = const.tile([P, S], F32, name="junk")
 
         v_grp = [const.tile([P, 2, D, 4], BF16, name="v_grp%d" % h, align_bytes=64) for h in range(H)]
-        v_code = [const.tile([P, 2 * D], U32, name="v_code%d" % h, align_bytes=64) for h in range(H)]
-        v_scale = [const.tile([P, 2 * D], U8, name="v_scale%d" % h, align_bytes=64) for h in range(H)]
+        v_code = const.tile([P, 2 * H * D], U32, name="v_code", align_bytes=64)
+        v_scale = const.tile([P, 2 * H * D], U8, name="v_scale", align_bytes=64)
+        nc.vector.memset(v_code[:].bitcast(I32), 0)
+        nc.vector.memset(v_scale[:].bitcast(I32), 0)
 
         def regroup_v(h):
             for g in range(2):
@@ -122,11 +124,13 @@ def tile_gpsdpattention_kernel(tc, Q, K, V, attn_mask, out):
                 )
 
         def quantise_v(h):
-            nc.vector.quantize_mx(
-                out=v_code[h][:].bitcast(FP8X4),
-                scales=v_scale[h][:],
-                in_=v_grp[h][:].rearrange("p g d t -> p (g d t)"),
-            )
+            for g in range(2):
+                col = (g * H + h) * D
+                nc.vector.quantize_mx(
+                    out=v_code[:, col : col + D].bitcast(FP8X4),
+                    scales=v_scale[:, col : col + D],
+                    in_=v_grp[h][:, g, :, :].rearrange("p d t -> p (d t)"),
+                )
 
         q_t = [const.tile([P, S], BF16, name="q_t%d" % h) for h in range(H)]
         k_t = [const.tile([P, S], BF16, name="k_t%d" % h) for h in range(H)]
@@ -234,35 +238,40 @@ def tile_gpsdpattention_kernel(tc, Q, K, V, attn_mask, out):
         finished = []
 
         def weighted(n):
-            h = n // NB
-            gi, n0, size, k = group_of[n]
-            if k == 0:
-                state["po"] = ps_o.tile([P, 4, D], F32, name="po", tag="o")
-            po = state["po"]
+            po = ps_o.tile([P, H * D], F32, name="po", tag="o")
             cd, sc = state[("cd", n)]
             for g in range(2):
                 nc.tensor.matmul_mx(
-                    out=po[:, k, :],
+                    out=po[:],
                     lhsT=cd[:, g * P : (g + 1) * P].bitcast(FP8X4),
                     lhsT_scale=sc[:, g * P : (g + 1) * P],
-                    rhs=v_code[h][:, g * D : (g + 1) * D].bitcast(FP8X4),
-                    rhs_scale=v_scale[h][:, g * D : (g + 1) * D],
+                    rhs=v_code[:, g * H * D : (g + 1) * H * D].bitcast(FP8X4),
+                    rhs_scale=v_scale[:, g * H * D : (g + 1) * H * D],
                     start=(g == 0),
                     stop=(g == 1),
                 )
+            state[("po", n)] = po
+
+        def invert(n):
+            gi, n0, size, k = group_of[n]
+            if k == size - 1:
+                nc.vector.reciprocal(out=row_inv[:, n0 : n0 + size], in_=row_sum[:, n0 : n0 + size])
 
         def finish(n):
+            h = n // NB
             gi, n0, size, k = group_of[n]
-            if k != size - 1:
-                return
-            po = state["po"]
-            nc.vector.reciprocal(out=row_inv[:, n0 : n0 + size], in_=row_sum[:, n0 : n0 + size])
-            ot = const.tile([P, size, D], F32, name="ot%d" % gi)
-            for j in range(size):
-                nc.scalar.activation(
-                    out=ot[:, j, :], in_=po[:, j, :], func=ACT.Copy, scale=row_inv[:, n0 + j : n0 + j + 1]
-                )
-            finished.append((n0, size, ot))
+            if k == 0:
+                state["ot"] = const.tile([P, size, D], F32, name="ot%d" % gi)
+            ot = state["ot"]
+            nc.scalar.activation(
+                out=ot[:, k, :], in_=state[("po", n)][:, h * D : (h + 1) * D], func=ACT.Copy, scale=row_inv[:, n : n + 1]
+            )
+            if k == size - 1:
+                finished.append((n0, size, ot))
+
+        def finish_step(n):
+            gi, n0, size, k = group_of[n]
+            return max(n + 3, n0 + size)
 
         make_prior(0)
         flip_in(k_raw[0], k_t[0], 0, True)
@@ -272,7 +281,7 @@ def tile_gpsdpattention_kernel(tc, Q, K, V, attn_mask, out):
         scores(0)
         flip_in(q_raw[0], q_t[0], 1, False)
         stored = 0
-        for t in range(NBLK + 3):
+        for t in range(NBLK + 4):
             if t + 1 < NBLK:
                 scores(t + 1)
             if t < NBLK:
@@ -284,16 +293,18 @@ def tile_gpsdpattention_kernel(tc, Q, K, V, attn_mask, out):
                     load_mask(nxt)
             if 0 <= t - 1 < NBLK:
                 flip(t - 1)
-            if 0 <= t - 3:
+            if 0 <= t - 3 < NBLK:
                 quant(t - 3)
                 weighted(t - 3)
             if t < NBLK:
                 row_max(t)
                 exps(t)
             if 0 <= t - 1 < NBLK:
+                invert(t - 1)
                 regroup(t - 1)
-            if 0 <= t - 3:
-                finish(t - 3)
+            for n in (t - 4, t - 3):
+                if 0 <= n < NBLK and finish_step(n) == t:
+                    finish(n)
             if t == 0:
                 quantise_v(0)
             if t + 1 < H:

@@ -104,13 +104,11 @@ def tile_gpsdpattention_kernel(tc, Q, K, V, attn_mask, out):
         neg_max = const.tile([P, NBLK], F32, name="neg_max")
         row_sum = const.tile([P, NBLK], F32, name="row_sum")
         row_inv = const.tile([P, NBLK], F32, name="row_inv")
-        junk = const.tile([P, S], F32, name="junk")
+        raw_max = const.tile([P, NBLK], F32, name="raw_max")
 
         v_grp = [const.tile([P, 2, D, 4], BF16, name="v_grp%d" % h, align_bytes=64) for h in range(H)]
-        v_code = const.tile([P, 2 * H * D], U32, name="v_code", align_bytes=64)
-        v_scale = const.tile([P, 2 * H * D], U8, name="v_scale", align_bytes=64)
-        nc.vector.memset(v_code[:].bitcast(I32), 0)
-        nc.vector.memset(v_scale[:].bitcast(I32), 0)
+        v_code = [const.tile([P, 2 * D], U32, name="v_code%d" % h, align_bytes=64) for h in range(H)]
+        v_scale = [const.tile([P, 2 * D], U8, name="v_scale%d" % h, align_bytes=64) for h in range(H)]
 
         def regroup_v(h):
             for g in range(2):
@@ -124,13 +122,11 @@ def tile_gpsdpattention_kernel(tc, Q, K, V, attn_mask, out):
                 )
 
         def quantise_v(h):
-            for g in range(2):
-                col = (g * H + h) * D
-                nc.vector.quantize_mx(
-                    out=v_code[:, col : col + D].bitcast(FP8X4),
-                    scales=v_scale[:, col : col + D],
-                    in_=v_grp[h][:, g, :, :].rearrange("p d t -> p (d t)"),
-                )
+            nc.vector.quantize_mx(
+                out=v_code[h][:].bitcast(FP8X4),
+                scales=v_scale[h][:],
+                in_=v_grp[h][:].rearrange("p g d t -> p (g d t)"),
+            )
 
         q_t = [const.tile([P, S], BF16, name="q_t%d" % h) for h in range(H)]
         k_t = [const.tile([P, S], BF16, name="k_t%d" % h) for h in range(H)]
@@ -185,14 +181,14 @@ def tile_gpsdpattention_kernel(tc, Q, K, V, attn_mask, out):
             state[("st", n)] = st
 
         def row_max(n):
-            nc.vector.tensor_scalar(
-                out=junk[:],
-                in0=state[("st", n)][:],
+            nc.vector.tensor_reduce(out=raw_max[:, n : n + 1], in_=state[("st", n)][:], axis=mybir.AxisListType.X, op=ALU.max)
+            nc.gpsimd.tensor_scalar(
+                out=neg_max[:, n : n + 1],
+                in0=raw_max[:, n : n + 1],
                 scalar1=-SCALE,
-                scalar2=None,
+                scalar2=0.0,
                 op0=ALU.mult,
-                op1=ALU.min,
-                accum_out=neg_max[:, n : n + 1],
+                op1=ALU.add,
             )
 
         def exps(n):
@@ -238,40 +234,35 @@ def tile_gpsdpattention_kernel(tc, Q, K, V, attn_mask, out):
         finished = []
 
         def weighted(n):
-            po = ps_o.tile([P, H * D], F32, name="po", tag="o")
-            cd, sc = state[("cd", n)]
-            for g in range(2):
-                nc.tensor.matmul_mx(
-                    out=po[:],
-                    lhsT=cd[:, g * P : (g + 1) * P].bitcast(FP8X4),
-                    lhsT_scale=sc[:, g * P : (g + 1) * P],
-                    rhs=v_code[:, g * H * D : (g + 1) * H * D].bitcast(FP8X4),
-                    rhs_scale=v_scale[:, g * H * D : (g + 1) * H * D],
-                    start=(g == 0),
-                    stop=(g == 1),
-                )
-            state[("po", n)] = po
-
-        def invert(n):
-            gi, n0, size, k = group_of[n]
-            if k == size - 1:
-                nc.vector.reciprocal(out=row_inv[:, n0 : n0 + size], in_=row_sum[:, n0 : n0 + size])
-
-        def finish(n):
             h = n // NB
             gi, n0, size, k = group_of[n]
             if k == 0:
-                state["ot"] = const.tile([P, size, D], F32, name="ot%d" % gi)
-            ot = state["ot"]
-            nc.scalar.activation(
-                out=ot[:, k, :], in_=state[("po", n)][:, h * D : (h + 1) * D], func=ACT.Copy, scale=row_inv[:, n : n + 1]
-            )
-            if k == size - 1:
-                finished.append((n0, size, ot))
+                state["po"] = ps_o.tile([P, 4, D], F32, name="po", tag="o")
+            po = state["po"]
+            cd, sc = state[("cd", n)]
+            for g in range(2):
+                nc.tensor.matmul_mx(
+                    out=po[:, k, :],
+                    lhsT=cd[:, g * P : (g + 1) * P].bitcast(FP8X4),
+                    lhsT_scale=sc[:, g * P : (g + 1) * P],
+                    rhs=v_code[h][:, g * D : (g + 1) * D].bitcast(FP8X4),
+                    rhs_scale=v_scale[h][:, g * D : (g + 1) * D],
+                    start=(g == 0),
+                    stop=(g == 1),
+                )
 
-        def finish_step(n):
+        def finish(n):
             gi, n0, size, k = group_of[n]
-            return max(n + 3, n0 + size)
+            if k != size - 1:
+                return
+            po = state["po"]
+            nc.vector.reciprocal(out=row_inv[:, n0 : n0 + size], in_=row_sum[:, n0 : n0 + size])
+            ot = const.tile([P, size, D], F32, name="ot%d" % gi)
+            for j in range(size):
+                nc.scalar.activation(
+                    out=ot[:, j, :], in_=po[:, j, :], func=ACT.Copy, scale=row_inv[:, n0 + j : n0 + j + 1]
+                )
+            finished.append((n0, size, ot))
 
         make_prior(0)
         flip_in(k_raw[0], k_t[0], 0, True)
@@ -281,7 +272,7 @@ def tile_gpsdpattention_kernel(tc, Q, K, V, attn_mask, out):
         scores(0)
         flip_in(q_raw[0], q_t[0], 1, False)
         stored = 0
-        for t in range(NBLK + 4):
+        for t in range(NBLK + 3):
             if t + 1 < NBLK:
                 scores(t + 1)
             if t < NBLK:
@@ -293,18 +284,16 @@ def tile_gpsdpattention_kernel(tc, Q, K, V, attn_mask, out):
                     load_mask(nxt)
             if 0 <= t - 1 < NBLK:
                 flip(t - 1)
-            if 0 <= t - 3 < NBLK:
+            if 0 <= t - 3:
                 quant(t - 3)
                 weighted(t - 3)
             if t < NBLK:
                 row_max(t)
                 exps(t)
             if 0 <= t - 1 < NBLK:
-                invert(t - 1)
                 regroup(t - 1)
-            for n in (t - 4, t - 3):
-                if 0 <= n < NBLK and finish_step(n) == t:
-                    finish(n)
+            if 0 <= t - 3:
+                finish(t - 3)
             if t == 0:
                 quantise_v(0)
             if t + 1 < H:

@@ -42,6 +42,8 @@ def tile_gpsdpattention_kernel(tc, Q, K, V, attn_mask, out):
 
     q_view = Q.rearrange("o h (b p) d -> p (o h b) d", p=P)
     k_view = K.rearrange("o h (b p) d -> p (o h b) d", p=P)
+    q_long = Q.rearrange("o h (p r) d -> p (o h) r d", p=P)
+    k_long = K.rearrange("o h (p r) d -> p (o h) r d", p=P)
     v_view = V.rearrange("o h (a p e) d -> p (o h a) (e d)", p=P, e=2)
     m_view = attn_mask.bitcast(I32).rearrange("o h (ib p) w -> p (o h ib) w", p=P)
     o_view = out.rearrange("o h (ib p) d -> p (o h ib) d", p=P)
@@ -58,12 +60,16 @@ def tile_gpsdpattention_kernel(tc, Q, K, V, attn_mask, out):
 
         def load_mask(n):
             mk = mask_pool.tile([P, 2 * S], I32, name="mk", tag="mk")
-            nc.sync.dma_start(out=mk[:], in_=m_view[:, n, :])
+            if n == NBLK - 1:
+                nc.sync.dma_start(out=mk[:, :S], in_=m_view[:, n, :S])
+                nc.sync.dma_start(out=mk[:, S:], in_=m_view[:, n, S:])
+            else:
+                nc.sync.dma_start(out=mk[:], in_=m_view[:, n, :])
             state[("mk", n)] = mk
 
         def load_qk(h):
-            nc.sync.dma_start(out=k_raw[h][:], in_=k_view[:, NB * h : NB * (h + 1), :])
-            nc.sync.dma_start(out=q_raw[h][:], in_=q_view[:, NB * h : NB * (h + 1), :])
+            nc.sync.dma_start(out=k_raw[h][:], in_=k_long[:, h, :, :])
+            nc.sync.dma_start(out=q_raw[h][:], in_=q_long[:, h, :, :])
             nc.sync.dma_start(out=v_raw[h][:], in_=v_view[:, 4 * h : 4 * h + 4, :])
 
         nc.sync.dma_start(out=k_raw[0][:], in_=k_view[:, 0:NB, :])
@@ -104,7 +110,7 @@ def tile_gpsdpattention_kernel(tc, Q, K, V, attn_mask, out):
         neg_max = const.tile([P, NBLK], F32, name="neg_max")
         row_sum = const.tile([P, NBLK], F32, name="row_sum")
         row_inv = const.tile([P, NBLK], F32, name="row_inv")
-        raw_max = const.tile([P, NBLK], F32, name="raw_max")
+        junk = const.tile([P, S], F32, name="junk")
 
         v_grp = [const.tile([P, 2, D, 4], BF16, name="v_grp%d" % h, align_bytes=64) for h in range(H)]
         v_code = [const.tile([P, 2 * D], U32, name="v_code%d" % h, align_bytes=64) for h in range(H)]
@@ -139,6 +145,15 @@ def tile_gpsdpattention_kernel(tc, Q, K, V, attn_mask, out):
                 nc.vector.tensor_copy(out=dst[:, 512 * half : 512 * (half + 1)], in_=pin[:])
             else:
                 nc.scalar.copy(out=dst[:, 512 * half : 512 * (half + 1)], in_=pin[:])
+
+        def flip_long(raw, dst):
+            pin = ps_t.tile([P, S], BF16, name="pin8", tag="t")
+            for r in range(NB):
+                nc.tensor.transpose(pin[:, r * P : (r + 1) * P], raw[:, r, :], ident_b[:])
+            nc.scalar.copy(
+                out=dst[:].rearrange("d (p r) -> d p r", r=NB),
+                in_=pin[:].rearrange("d (r p) -> d p r", r=NB),
+            )
 
         def scores(n):
             h, ib = divmod(n, NB)
@@ -181,14 +196,14 @@ def tile_gpsdpattention_kernel(tc, Q, K, V, attn_mask, out):
             state[("st", n)] = st
 
         def row_max(n):
-            nc.vector.tensor_reduce(out=raw_max[:, n : n + 1], in_=state[("st", n)][:], axis=mybir.AxisListType.X, op=ALU.max)
-            nc.gpsimd.tensor_scalar(
-                out=neg_max[:, n : n + 1],
-                in0=raw_max[:, n : n + 1],
+            nc.vector.tensor_scalar(
+                out=junk[:],
+                in0=state[("st", n)][:],
                 scalar1=-SCALE,
-                scalar2=0.0,
+                scalar2=None,
                 op0=ALU.mult,
-                op1=ALU.add,
+                op1=ALU.min,
+                accum_out=neg_max[:, n : n + 1],
             )
 
         def exps(n):
@@ -305,11 +320,10 @@ def tile_gpsdpattention_kernel(tc, Q, K, V, attn_mask, out):
                 if (t + 5) % NB == 2:
                     quantise_v(h_next)
             h_flip, piece = divmod(t + 5, NB)
-            if 0 < h_flip < H and piece < 4:
-                if piece % 2 == 0:
-                    flip_in(k_raw[h_flip], k_t[h_flip], piece // 2, False)
-                else:
-                    flip_in(q_raw[h_flip], q_t[h_flip], piece // 2, False)
+            if 0 < h_flip < H and piece == 0:
+                flip_long(k_raw[h_flip], k_t[h_flip])
+            if 0 < h_flip < H and piece == 2:
+                flip_long(q_raw[h_flip], q_t[h_flip])
             if t + MASK_BUFS >= NBLK - 1:
                 for n0, size, ot in finished[stored:]:
                     nc.sync.dma_start(out=o_view[:, n0 : n0 + size, :], in_=ot[:])

@@ -110,7 +110,7 @@ def tile_gpsdpattention_kernel(tc, Q, K, V, attn_mask, out):
         neg_max = const.tile([P, NBLK], F32, name="neg_max")
         row_sum = const.tile([P, NBLK], F32, name="row_sum")
         row_inv = const.tile([P, NBLK], F32, name="row_inv")
-        junk = const.tile([P, S], F32, name="junk")
+        raw_max = const.tile([P, NBLK], F32, name="raw_max")
 
         v_grp = [const.tile([P, 2, D, 4], BF16, name="v_grp%d" % h, align_bytes=64) for h in range(H)]
         v_code = [const.tile([P, 2 * D], U32, name="v_code%d" % h, align_bytes=64) for h in range(H)]
@@ -196,14 +196,14 @@ def tile_gpsdpattention_kernel(tc, Q, K, V, attn_mask, out):
             state[("st", n)] = st
 
         def row_max(n):
-            nc.vector.tensor_scalar(
-                out=junk[:],
-                in0=state[("st", n)][:],
+            nc.vector.tensor_reduce(out=raw_max[:, n : n + 1], in_=state[("st", n)][:], axis=mybir.AxisListType.X, op=ALU.max)
+            nc.gpsimd.tensor_scalar(
+                out=neg_max[:, n : n + 1],
+                in0=raw_max[:, n : n + 1],
                 scalar1=-SCALE,
-                scalar2=None,
+                scalar2=0.0,
                 op0=ALU.mult,
-                op1=ALU.min,
-                accum_out=neg_max[:, n : n + 1],
+                op1=ALU.add,
             )
 
         def exps(n):

import math

import concourse.mybir as mybir
from concourse.masks import make_identity

F32 = mybir.dt.float32
BF16 = mybir.dt.bfloat16
I32 = mybir.dt.int32
U32 = mybir.dt.uint32
U8 = mybir.dt.uint8
FP8X4 = mybir.dt.float8_e4m3fn_x4
ALU = mybir.AluOpType
ACT = mybir.ActivationFunctionType

P = 128
H = 4
S = 1024
D = 128
NB = S // P
NBLK = H * NB
SIGMA = (5.0, 10.0, 20.0, 40.0)
FLOPS = 2 * 2 * H * S * S * D

SCALE = 1.0 / math.sqrt(D)
MASKED = -1.0e9 * math.sqrt(D)
CUT = 30.0
MASK_BUFS = 10
GROUPS = (4, 4, 4, 4, 4, 4, 4, 2, 1, 1)


def prior_deltas(h):
    keep = []
    for delta in range(0, S, P):
        low = delta - (P - 1)
        if low <= 0 or low * low / (2.0 * SIGMA[h] ** 2) < CUT:
            keep.append(delta)
    return keep


def tile_gpsdpattention_kernel(tc, Q, K, V, attn_mask, out):
    nc = tc.nc

    q_view = Q.rearrange("o h (b p) d -> p (o h b) d", p=P)
    k_view = K.rearrange("o h (b p) d -> p (o h b) d", p=P)
    q_long = Q.rearrange("o h (p r) d -> p (o h) r d", p=P)
    k_long = K.rearrange("o h (p r) d -> p (o h) r d", p=P)
    v_view = V.rearrange("o h (a p e) d -> p (o h a) (e d)", p=P, e=2)
    m_view = attn_mask.bitcast(I32).rearrange("o h (ib p) w -> p (o h ib) w", p=P)
    o_view = out.rearrange("o h (ib p) d -> p (o h ib) d", p=P)

    with tc.tile_pool(name="const", bufs=1) as const, tc.tile_pool(name="work", bufs=3) as work, tc.tile_pool(
        name="masks", bufs=MASK_BUFS
    ) as mask_pool, tc.psum_pool(name="ps_s", bufs=2) as ps_s, tc.psum_pool(name="ps_t", bufs=2) as ps_t, tc.psum_pool(
        name="ps_o", bufs=2
    ) as ps_o, tc.manual_schedule():
        state = {}
        k_raw = [const.tile([P, NB, D], BF16, name="k_raw%d" % h) for h in range(H)]
        q_raw = [const.tile([P, NB, D], BF16, name="q_raw%d" % h) for h in range(H)]
        v_raw = [const.tile([P, 4, 2 * D], BF16, name="v_raw%d" % h) for h in range(H)]

        def load_mask(n):
            mk = mask_pool.tile([P, 2 * S], I32, name="mk", tag="mk")
            if n == NBLK - 1:
                nc.sync.dma_start(out=mk[:, :S], in_=m_view[:, n, :S])
                nc.sync.dma_start(out=mk[:, S:], in_=m_view[:, n, S:])
            else:
                nc.sync.dma_start(out=mk[:], in_=m_view[:, n, :])
            state[("mk", n)] = mk

        def load_qk(h):
            nc.sync.dma_start(out=k_raw[h][:], in_=k_long[:, h, :, :])
            nc.sync.dma_start(out=q_raw[h][:], in_=q_long[:, h, :, :])
            nc.sync.dma_start(out=v_raw[h][:], in_=v_view[:, 4 * h : 4 * h + 4, :])

        nc.sync.dma_start(out=k_raw[0][:], in_=k_view[:, 0:NB, :])
        nc.scalar.dma_start(out=q_raw[0][:], in_=q_view[:, 0:NB, :])
        load_mask(0)
        nc.sync.dma_start(out=v_raw[0][:], in_=v_view[:, 0:4, :])
        for n in range(1, 3):
            load_mask(n)
        load_qk(1)
        for n in range(3, MASK_BUFS):
            load_mask(n)

        ident_b = const.tile([P, P], BF16, name="ident_b")
        make_identity(nc, ident_b[:])
        width = max(prior_deltas(H - 1)) + P
        dist = const.tile([P, width], F32, name="dist")
        nc.gpsimd.iota(dist[:], pattern=[[1, width]], base=0, channel_multiplier=-1, allow_small_or_imprecise_dtypes=True)
        ident_f = const.tile([P, P], F32, name="ident_f")
        make_identity(nc, ident_f[:])
        dist_p = const.tile([P, width], F32, name="dist_p")
        nc.vector.scalar_tensor_tensor(out=dist_p[:], in0=dist[:], scalar=-1.0e4, in1=dist[:], op0=ALU.mult, op1=ALU.max)
        dist_2 = const.tile([P, width], F32, name="dist_2")
        nc.scalar.activation(out=dist_2[:], in_=dist_p[:], func=ACT.Square)
        prior = [const.tile([P, max(prior_deltas(h)) + P], F32, name="prior%d" % h) for h in range(H)]

        def make_prior(h):
            w_h = max(prior_deltas(h)) + P
            nc.scalar.activation(out=prior[h][:], in_=dist_2[:, :w_h], func=ACT.Exp, scale=-1.0 / (2.0 * SIGMA[h] ** 2))
            if h == 0:
                nc.vector.tensor_scalar(
                    out=prior[h][:], in0=prior[h][:], scalar1=math.sqrt(D), scalar2=None, op0=ALU.mult
                )
            else:
                nc.gpsimd.tensor_scalar(
                    out=prior[h][:], in0=prior[h][:], scalar1=math.sqrt(D), scalar2=0.0, op0=ALU.mult, op1=ALU.add
                )

        neg_max = const.tile([P, NBLK], F32, name="neg_max")
        row_sum = const.tile([P, NBLK], F32, name="row_sum")
        row_inv = const.tile([P, NBLK], F32, name="row_inv")
        raw_max = const.tile([P, NBLK], F32, name="raw_max")

        v_grp = [const.tile([P, 2, D, 4], BF16, name="v_grp%d" % h, align_bytes=64) for h in range(H)]
        v_code = [const.tile([P, 2 * D], U32, name="v_code%d" % h, align_bytes=64) for h in range(H)]
        v_scale = [const.tile([P, 2 * D], U8, name="v_scale%d" % h, align_bytes=64) for h in range(H)]

        def regroup_v(h):
            for g in range(2):
                nc.gpsimd.tensor_scalar(
                    out=v_grp[h][:, g, :, :].rearrange("p d (u e) -> p d u e", u=2),
                    in0=v_raw[h][:, 2 * g : 2 * g + 2, :].rearrange("p u (e d) -> p d u e", e=2),
                    scalar1=1.0,
                    scalar2=0.0,
                    op0=ALU.mult,
                    op1=ALU.add,
                )

        def quantise_v(h):
            nc.vector.quantize_mx(
                out=v_code[h][:].bitcast(FP8X4),
                scales=v_scale[h][:],
                in_=v_grp[h][:].rearrange("p g d t -> p (g d t)"),
            )

        q_t = [const.tile([P, S], BF16, name="q_t%d" % h) for h in range(H)]
        k_t = [const.tile([P, S], BF16, name="k_t%d" % h) for h in range(H)]

        def flip_in(raw, dst, half, on_vector):
            pin = ps_t.tile([P, 512], BF16, name="pin", tag="t")
            for b in range(4):
                nc.tensor.transpose(pin[:, b * P : (b + 1) * P], raw[:, 4 * half + b, :], ident_b[:])
            if on_vector:
                nc.vector.tensor_copy(out=dst[:, 512 * half : 512 * (half + 1)], in_=pin[:])
            else:
                nc.scalar.copy(out=dst[:, 512 * half : 512 * (half + 1)], in_=pin[:])

        def flip_long(raw, dst):
            pin = ps_t.tile([P, S], BF16, name="pin8", tag="t")
            for r in range(NB):
                nc.tensor.transpose(pin[:, r * P : (r + 1) * P], raw[:, r, :], ident_b[:])
            nc.scalar.copy(
                out=dst[:].rearrange("d (p r) -> d p r", r=NB),
                in_=pin[:].rearrange("d (r p) -> d p r", r=NB),
            )

        def scores(n):
            h, ib = divmod(n, NB)
            banks = []
            for pl in range(2):
                ps = ps_s.tile([P, 512], F32, name="ps%d" % pl, tag="s%d" % pl)
                adds = [b for b in range(4) if P * (ib - 4 * pl - b) in prior_deltas(h)]
                nc.tensor.matmul(
                    ps[:],
                    lhsT=q_t[h][:, ib * P : (ib + 1) * P],
                    rhs=k_t[h][:, pl * 512 : (pl + 1) * 512],
                    start=True,
                    stop=(len(adds) == 0),
                )
                for b in adds:
                    x0 = P * (ib - 4 * pl - b)
                    nc.tensor.matmul(
                        ps[:, b * P : (b + 1) * P],
                        lhsT=prior[h][:, x0 : x0 + P],
                        rhs=ident_f[:],
                        is_transpose=True,
                        start=False,
                        stop=(b == adds[-1]),
                    )
                banks.append(ps)
            state[("ps", n)] = banks

        def masked(n):
            st = work.tile([P, S], F32, name="st", tag="st")
            low_words = state[("mk", n)][:].rearrange("p (c f) -> p c f", f=2)
            for pl in range(2):
                nc.vector.scalar_tensor_tensor(
                    out=st[:, pl * 512 : (pl + 1) * 512],
                    in0=low_words[:, pl * 512 : (pl + 1) * 512, 0],
                    scalar=MASKED,
                    in1=state[("ps", n)][pl][:],
                    op0=ALU.mult,
                    op1=ALU.add,
                )
            state[("st", n)] = st

        def row_max(n):
            nc.vector.tensor_reduce(out=raw_max[:, n : n + 1], in_=state[("st", n)][:], axis=mybir.AxisListType.X, op=ALU.max)
            nc.gpsimd.tensor_scalar(
                out=neg_max[:, n : n + 1],
                in0=raw_max[:, n : n + 1],
                scalar1=-SCALE,
                scalar2=0.0,
                op0=ALU.mult,
                op1=ALU.add,
            )

        def exps(n):
            et = work.tile([P, S], BF16, name="et", tag="et")
            nc.scalar.activation(
                out=et[:],
                in_=state[("st", n)][:],
                func=ACT.Exp,
                bias=neg_max[:, n : n + 1],
                scale=SCALE,
                accum_out=row_sum[:, n : n + 1],
            )
            state[("et", n)] = et

        def flip(n):
            pt = ps_t.tile([P, 4, P], F32, name="pt", tag="t")
            words = state[("et", n)][:].bitcast(F32)
            for beta in range(4):
                nc.tensor.transpose(pt[:, beta, :], words[:, beta * P : (beta + 1) * P], ident_f[:])
            state[("pt", n)] = pt

        def regroup(n):
            gt = work.tile([P, 2, P, 2], F32, name="gt", tag="gt", bufs=4, align_bytes=64)
            nc.scalar.copy(out=gt[:], in_=state[("pt", n)][:].rearrange("p (g u) i -> p g i u", u=2))
            state[("gt", n)] = gt

        def quant(n):
            cd = work.tile([P, 2 * P], U32, name="cd", tag="cd", align_bytes=64)
            sc = work.tile([P, 2 * P], U8, name="sc", tag="sc", align_bytes=64)
            nc.vector.quantize_mx(
                out=cd[:].bitcast(FP8X4),
                scales=sc[:],
                in_=state[("gt", n)][:].rearrange("p g i u -> p (g i u)").bitcast(BF16),
            )
            state[("cd", n)] = (cd, sc)

        group_of = {}
        first = 0
        for gi, size in enumerate(GROUPS):
            for k in range(size):
                group_of[first + k] = (gi, first, size, k)
            first += size
        finished = []

        def weighted(n):
            h = n // NB
            gi, n0, size, k = group_of[n]
            if k == 0:
                state["po"] = ps_o.tile([P, 4, D], F32, name="po", tag="o")
            po = state["po"]
            cd, sc = state[("cd", n)]
            for g in range(2):
                nc.tensor.matmul_mx(
                    out=po[:, k, :],
                    lhsT=cd[:, g * P : (g + 1) * P].bitcast(FP8X4),
                    lhsT_scale=sc[:, g * P : (g + 1) * P],
                    rhs=v_code[h][:, g * D : (g + 1) * D].bitcast(FP8X4),
                    rhs_scale=v_scale[h][:, g * D : (g + 1) * D],
                    start=(g == 0),
                    stop=(g == 1),
                )

        def finish(n):
            gi, n0, size, k = group_of[n]
            if k != size - 1:
                return
            po = state["po"]
            nc.vector.reciprocal(out=row_inv[:, n0 : n0 + size], in_=row_sum[:, n0 : n0 + size])
            ot = const.tile([P, size, D], F32, name="ot%d" % gi)
            for j in range(size):
                nc.scalar.activation(
                    out=ot[:, j, :], in_=po[:, j, :], func=ACT.Copy, scale=row_inv[:, n0 + j : n0 + j + 1]
                )
            finished.append((n0, size, ot))

        make_prior(0)
        flip_in(k_raw[0], k_t[0], 0, True)
        flip_in(q_raw[0], q_t[0], 0, False)
        flip_in(k_raw[0], k_t[0], 1, True)
        regroup_v(0)
        scores(0)
        flip_in(q_raw[0], q_t[0], 1, False)
        stored = 0
        for t in range(NBLK + 3):
            if t + 1 < NBLK:
                scores(t + 1)
            if t < NBLK:
                masked(t)
                nxt = t + MASK_BUFS
                if nxt < NBLK:
                    if nxt % NB == NB - 4 and nxt // NB + 1 < H:
                        load_qk(nxt // NB + 1)
                    load_mask(nxt)
            if 0 <= t - 1 < NBLK:
                flip(t - 1)
            if 0 <= t - 3:
                quant(t - 3)
                weighted(t - 3)
            if t < NBLK:
                row_max(t)
                exps(t)
            if 0 <= t - 1 < NBLK:
                regroup(t - 1)
            if 0 <= t - 3:
                finish(t - 3)
            if t == 0:
                quantise_v(0)
            if t + 1 < H:
                make_prior(t + 1)
            h_next = (t + 5) // NB
            if 0 < h_next < H:
                if (t + 5) % NB == 0:
                    regroup_v(h_next)
                if (t + 5) % NB == 2:
                    quantise_v(h_next)
            h_flip, piece = divmod(t + 5, NB)
            if 0 < h_flip < H and piece == 0:
                flip_long(k_raw[h_flip], k_t[h_flip])
            if 0 < h_flip < H and piece == 2:
                flip_long(q_raw[h_flip], q_t[h_flip])
            if t + MASK_BUFS >= NBLK - 1:
                for n0, size, ot in finished[stored:]:
                    nc.sync.dma_start(out=o_view[:, n0 : n0 + size, :], in_=ot[:])
                stored = len(finished)
